import numpy as np
import ml_dtypes


def mxq(x, axis, fmt="e4m3"):
    dtype, down = {"e4m3": (ml_dtypes.float8_e4m3fn, 7), "e5m2": (ml_dtypes.float8_e5m2, 14)}[fmt]
    v = np.moveaxis(np.asarray(x, np.float32).astype(ml_dtypes.bfloat16).astype(np.float64), axis, -1)
    blocks = v.reshape(v.shape[:-1] + (-1, 32))
    amax = np.abs(blocks).max(-1, keepdims=True)
    byte = np.maximum(np.where(amax > 0, np.frexp(amax)[1] - 1 + 127, 0) - down, 1)
    scale = np.exp2(byte - 127.0)
    codes = (blocks / scale).astype(np.float32).astype(dtype).astype(np.float64)
    return np.moveaxis((codes * scale).reshape(v.shape), -1, axis)


WIDE = False


def mx_kscale(k):
    if not WIDE:
        return np.ones(k)
    levels = np.array([10, -10, 5, -5, 0])
    a = np.random.permutation(np.resize(levels, k // 512 * 4)).reshape(k // 512, 4)
    idx = np.arange(k)
    return np.exp2(a[idx // 512, idx % 128 // 32])


BF16 = ml_dtypes.bfloat16


def bf(x):
    return np.asarray(x, np.float32).astype(BF16)


def f64(x):
    return np.asarray(x).astype(np.float64)


E2M1 = np.array([0.0, 0.5, 1.0, 1.5, 2.0, 3.0, 4.0, 6.0, -0.0, -0.5, -1.0, -1.5, -2.0, -3.0, -4.0, -6.0])


def pack_weight(w, fmt):
    k, n = w.shape
    w = f64(bf(w)).reshape(k // 32, 32, n)
    amax = np.abs(w).max(1)
    if fmt == "e4m3":
        byte = np.frexp(amax)[1] - 1 + 127 - 7
    else:
        mant, ex = np.frexp(amax / 6.0)
        byte = np.where(mant > 0.5, ex, ex - 1) + 127
    byte = np.clip(np.where(amax > 0, byte, 1), 1, 254)
    scaled = (w * np.exp2(127.0 - byte)[:, None, :]).reshape(k, n).astype(np.float32)
    by_word = np.ascontiguousarray(scaled.reshape(k // 512, 128, 4, n).transpose(0, 1, 3, 2))
    if fmt == "e4m3":
        words = by_word.astype(ml_dtypes.float8_e4m3fn).view(np.uint8)
    else:
        c = by_word.astype(ml_dtypes.float4_e2m1fn).view(np.uint8) & 0xF
        words = c[..., 0::2] | (c[..., 1::2] << 4)
    return np.ascontiguousarray(words), np.ascontiguousarray(byte.astype(np.uint8).reshape(k // 512, 16, n))


def unpack_weight(words, scales, fmt):
    g, p, n, _ = words.shape
    if fmt == "e4m3":
        vals = np.ascontiguousarray(words).view(ml_dtypes.float8_e4m3fn).astype(np.float64)
    else:
        nib = np.empty((g, p, n, 4), np.uint8)
        nib[..., 0::2] = words & 0xF
        nib[..., 1::2] = words >> 4
        vals = E2M1[nib]
    vals = vals * np.repeat(np.exp2(scales.astype(np.float64) - 127.0), 8, axis=1)[..., None]
    return vals.transpose(0, 1, 3, 2).reshape(g * 512, n)


B, C, MID, HH, WW = 4, 256, 1024, 32, 32
N = HH * WW


def setup_inputs():
    s, t = mx_kscale(N), mx_kscale(MID)
    a = np.exp(1.5 * np.random.standard_normal((B, N, N)))
    a = a / a.sum(-1, keepdims=True)
    attn = bf(a * s)
    h_x = bf(np.random.standard_normal((B, MID, N)) * 2.0 * t[:, None] / s)
    v_w = np.random.standard_normal((C, MID)) * 3.0 / np.sqrt(MID) / t
    v_w_words, v_w_scales = pack_weight(np.ascontiguousarray(v_w.T), "e4m3")
    return {
        "attn": attn,
        "h_x": h_x,
        "v_w_words": v_w_words,
        "v_w_scales": v_w_scales,
        "v_b": bf(np.random.standard_normal(C) * 0.3),
        "x": bf(np.random.standard_normal((B, C, HH, WW))),
    }


def reference(attn, h_x, v_w_words, v_w_scales, v_b, x):
    z = mxq(f64(h_x), 2, "e4m3") @ mxq(f64(attn), 2, "e4m3").transpose(0, 2, 1)
    y = (unpack_weight(v_w_words, v_w_scales, "e4m3").T @ mxq(z, 1, "e4m3")) + f64(v_b)[None, :, None]
    return y.reshape(B, C, HH, WW) + f64(x)

@@ -1,0 +1,227 @@
+from contextlib import ExitStack
+
+import concourse.mybir as mybir
+from concourse.masks import make_identity
+
+BF16 = mybir.dt.bfloat16
+F32 = mybir.dt.float32
+I32 = mybir.dt.int32
+U32 = mybir.dt.uint32
+U8 = mybir.dt.uint8
+FP8X4 = mybir.dt.float8_e4m3fn_x4
+ADD = mybir.AluOpType.add
+
+BATCH = 4
+OUT_CH = 256
+MID_CH = 1024
+POS = 1024
+
+P = 128
+PACK = 4
+K_PASS = P * PACK
+PASSES = POS // K_PASS
+BANK = 512
+
+QUARTER = 512
+ROW_TILES = QUARTER // P
+QUARTERS = 4 * BATCH
+ROUNDS = 4 * BATCH
+Y_GROUPS = 4 * BATCH
+
+TRANSPOSE_AHEAD = 2
+LOAD_AHEAD = 6
+PROJECT_BEHIND = 2
+
+FLOPS = 2 * BATCH * (MID_CH * POS * POS + OUT_CH * MID_CH * POS)
+
+
+def tile_soablock_pb_t_kernel(tc, attn, h_x, v_w_words, v_w_scales, v_b, x, out):
+    nc = tc.nc
+    x_rows = x.rearrange("b c h w -> b c (h w)")
+    out_rows = out.rearrange("b c h w -> b c (h w)")
+
+    with ExitStack() as stack:
+        const = stack.enter_context(tc.tile_pool(name="const", bufs=1))
+        raw_pool = stack.enter_context(tc.tile_pool(name="raw", bufs=LOAD_AHEAD + 2))
+        grouped_pool = stack.enter_context(tc.tile_pool(name="grouped", bufs=2))
+        codes_pool = stack.enter_context(tc.tile_pool(name="codes", bufs=6))
+        z_grouped_pool = stack.enter_context(tc.tile_pool(name="z_grouped", bufs=2))
+        z_codes_pool = stack.enter_context(tc.tile_pool(name="z_codes", bufs=4))
+        x_pool = stack.enter_context(tc.tile_pool(name="x", bufs=3))
+        result_pool = stack.enter_context(tc.tile_pool(name="result", bufs=3))
+        z_psum = stack.enter_context(tc.psum_pool(name="z_psum", bufs=3))
+        wide_psum = stack.enter_context(tc.psum_pool(name="wide_psum", bufs=5))
+        stack.enter_context(tc.manual_schedule())
+
+        raws, groupeds, codes, planes = {}, {}, {}, {}
+        z_groupeds, z_codes, z_planes = {}, {}, {}
+        x_tiles, y_banks = {}, {}
+
+        def load_quarter(q):
+            b, half = q // 4, (q % 4) // 2
+            rows = slice(half * QUARTER, (half + 1) * QUARTER)
+            if q % 2 == 0:
+                source = h_x[b, rows, :].rearrange("(p j) m -> p j m", j=ROW_TILES)
+            else:
+                source = attn[b, rows, :].rearrange("(r p) m -> p r m", p=P)
+            raw = raw_pool.tile([P, ROW_TILES, POS], BF16)
+            for pair in range(ROW_TILES // 2):
+                two = slice(2 * pair, 2 * pair + 2)
+                nc.sync.dma_start(out=raw[:, two, :], in_=source[:, two, :])
+            raws[q] = raw
+            if q % 4 == 3:
+                x_tile = x_pool.tile([P, OUT_CH // P, POS], BF16)
+                nc.sync.dma_start(out=x_tile[:], in_=x_rows[b].rearrange("(t p) n -> p t n", p=P))
+                x_tiles[b] = x_tile
+
+        def transpose_quarter(q):
+            raw = raws[q]
+            grouped = grouped_pool.tile([P, PASSES, QUARTER, PACK], BF16, align_bytes=64)
+            for pair in range(ROW_TILES // 2):
+                for k in range(PASSES):
+                    bank = wide_psum.tile([P, BANK], F32, tag="wide")
+                    for u in range(2):
+                        for r in range(2):
+                            words = raw[:, 2 * pair + r, :].bitcast(F32)
+                            first = (2 * k + u) * P
+                            nc.tensor.transpose(
+                                bank[:, (2 * u + r) * P : (2 * u + r + 1) * P],
+                                words[:, first : first + P],
+                                ident_f32[:],
+                            )
+                    rows = slice(2 * pair * P, (2 * pair + 2) * P)
+                    dest = grouped[:, k, rows, :].bitcast(F32)
+                    source = bank[:].rearrange("p (u r) -> p r u", u=2)
+                    if k == 0:
+                        nc.scalar.copy(out=dest, in_=source)
+                    else:
+                        nc.vector.tensor_copy(out=dest, in_=source)
+            groupeds[q] = grouped
+
+        def quantise_quarter(q):
+            grouped = groupeds[q]
+            code = codes_pool.tile([P, PASSES, QUARTER], U32, align_bytes=64)
+            plane = codes_pool.tile([P, PASSES, QUARTER], U8, align_bytes=64)
+            for k in range(PASSES):
+                nc.vector.quantize_mx(
+                    out=code[:, k, :].bitcast(FP8X4),
+                    scales=plane[:, k, :],
+                    in_=grouped[:, k, :, :].rearrange("p r t -> p (r t)"),
+                )
+            codes[q] = code
+            planes[q] = plane
+
+        def mix_round(i):
+            b, half, g = i // 4, (i % 4) // 2, i % 2
+            h_q, a_q = 4 * b + 2 * g, 4 * b + 2 * half + 1
+            z_grouped = z_grouped_pool.tile([P, QUARTER, PACK], BF16, align_bytes=64)
+            for chunk in range(QUARTER // P):
+                cols = slice(chunk * P, (chunk + 1) * P)
+                bank = z_psum.tile([P, PACK, P], F32)
+                for j in range(PACK):
+                    chans = slice(j * P, (j + 1) * P)
+                    for k in range(PASSES):
+                        nc.tensor.matmul_mx(
+                            out=bank[:, j, :],
+                            lhsT=codes[h_q][:, k, chans].bitcast(FP8X4),
+                            lhsT_scale=planes[h_q][:, k, chans],
+                            rhs=codes[a_q][:, k, cols].bitcast(FP8X4),
+                            rhs_scale=planes[a_q][:, k, cols],
+                            start=(k == 0),
+                            stop=(k == PASSES - 1),
+                        )
+                nc.scalar.copy(out=z_grouped[:, cols, :], in_=bank[:].rearrange("p j n -> p n j"))
+            z_groupeds[i] = z_grouped
+
+        def quantise_z(i):
+            z_code = z_codes_pool.tile([P, QUARTER], U32, align_bytes=64)
+            z_plane = z_codes_pool.tile([P, QUARTER], U8, align_bytes=64)
+            nc.vector.quantize_mx(
+                out=z_code[:].bitcast(FP8X4),
+                scales=z_plane[:],
+                in_=z_groupeds[i][:].rearrange("p n j -> p (n j)"),
+            )
+            z_codes[i] = z_code
+            z_planes[i] = z_plane
+
+        def project(y):
+            b, half, t = y // 4, (y % 4) // 2, y % 2
+            outs = slice(t * P, (t + 1) * P)
+            bank = wide_psum.tile([P, BANK], F32, tag="wide")
+            for g in range(PASSES):
+                i = 4 * b + 2 * half + g
+                nc.tensor.matmul_mx(
+                    out=bank[:],
+                    lhsT=w_words[:, g, outs].bitcast(FP8X4),
+                    lhsT_scale=w_plane[:, g, outs],
+                    rhs=z_codes[i][:].bitcast(FP8X4),
+                    rhs_scale=z_planes[i][:],
+                    start=(g == 0),
+                    stop=(g == PASSES - 1),
+                )
+            y_banks[y] = bank
+
+        def finish(y):
+            b, half, t = y // 4, (y % 4) // 2, y % 2
+            cols = slice(half * BANK, (half + 1) * BANK)
+            result = result_pool.tile([P, BANK], F32)
+            nc.vector.scalar_tensor_tensor(
+                out=result[:],
+                in0=y_banks[y][:],
+                scalar=bias[:, t : t + 1],
+                in1=x_tiles[b][:, t, cols],
+                op0=ADD,
+                op1=ADD,
+            )
+            nc.sync.dma_start(out=out_rows[b, t * P : (t + 1) * P, cols], in_=result[:])
+
+        ident_f32 = const.tile([P, P], F32)
+        make_identity(nc, ident_f32[:])
+        ident_bf16 = const.tile([P, P], BF16)
+        make_identity(nc, ident_bf16[:])
+
+        w_words = const.tile([P, PASSES, OUT_CH], U32, align_bytes=64)
+        w_plane = const.tile([P, PASSES, OUT_CH], U8, align_bytes=64)
+        nc.vector.memset(w_plane[:].bitcast(I32), 0)
+        bias_rows = const.tile([P, P], BF16)
+        nc.vector.memset(bias_rows[:], 0.0)
+
+        load_quarter(0)
+        load_quarter(1)
+        nc.sync.dma_start(out=bias_rows[0 : OUT_CH // P, :], in_=v_b.rearrange("(t p) -> t p", p=P))
+        load_quarter(2)
+        nc.sync.dma_start(
+            out=w_words[:].bitcast(I32),
+            in_=v_w_words.rearrange("g p o t -> p g (o t)").bitcast(I32),
+        )
+        for quad in range(4):
+            nc.sync.dma_start(
+                out=w_plane[32 * quad : 32 * quad + 4, :, :].bitcast(I32),
+                in_=v_w_scales[:, 4 * quad : 4 * quad + 4, :].rearrange("g r o -> r g o").bitcast(I32),
+            )
+        for q in range(3, LOAD_AHEAD):
+            load_quarter(q)
+
+        for q in range(TRANSPOSE_AHEAD):
+            transpose_quarter(q)
+            quantise_quarter(q)
+
+        bias_bank = wide_psum.tile([P, P], BF16, tag="wide")
+        nc.tensor.transpose(bias_bank[:], bias_rows[:], ident_bf16[:])
+        bias = const.tile([P, OUT_CH // P], F32)
+        nc.vector.tensor_copy(out=bias[:], in_=bias_bank[:, 0 : OUT_CH // P])
+
+        for i in range(ROUNDS + PROJECT_BEHIND + 1):
+            if i + LOAD_AHEAD < QUARTERS:
+                load_quarter(i + LOAD_AHEAD)
+            if 0 <= i - PROJECT_BEHIND - 1 < Y_GROUPS:
+                finish(i - PROJECT_BEHIND - 1)
+            if 0 <= i - 1 < ROUNDS:
+                quantise_z(i - 1)
+            if i + TRANSPOSE_AHEAD < QUARTERS:
+                transpose_quarter(i + TRANSPOSE_AHEAD)
+                quantise_quarter(i + TRANSPOSE_AHEAD)
+            if i < ROUNDS:
+                mix_round(i)
+            if 0 <= i - PROJECT_BEHIND < Y_GROUPS:
+                project(i - PROJECT_BEHIND)

@@ -27,6 +27,7 @@ ROW_TILES = QUARTER // P
 QUARTERS = 4 * BATCH
 ROUNDS = 4 * BATCH
 Y_GROUPS = 4 * BATCH
+Y_COLS = POS // 4
 
 TRANSPOSE_AHEAD = 2
 LOAD_AHEAD = 6
@@ -133,47 +134,54 @@ def tile_soablock_pb_t_kernel(tc, attn, h_x, v_w_words, v_w_scales, v_b, x, out)
                 nc.scalar.copy(out=z_grouped[:, cols, :], in_=bank[:].rearrange("p j n -> p n j"))
             z_groupeds[i] = z_grouped
 
-        def quantise_z(i):
-            z_code = z_codes_pool.tile([P, QUARTER], U32, align_bytes=64)
-            z_plane = z_codes_pool.tile([P, QUARTER], U8, align_bytes=64)
+        def quantise_z(i, part):
+            if part == 0:
+                z_code = z_codes_pool.tile([P, QUARTER], U32, align_bytes=64)
+                z_plane = z_codes_pool.tile([P, QUARTER], U8, align_bytes=64)
+                z_codes[i] = z_code
+                z_planes[i] = z_plane
+            cols = slice(part * Y_COLS, (part + 1) * Y_COLS)
             nc.vector.quantize_mx(
-                out=z_code[:].bitcast(FP8X4),
-                scales=z_plane[:],
-                in_=z_groupeds[i][:].rearrange("p n j -> p (n j)"),
+                out=z_codes[i][:, cols].bitcast(FP8X4),
+                scales=z_planes[i][:, cols],
+                in_=z_groupeds[i][:, cols, :].rearrange("p n j -> p (n j)"),
             )
-            z_codes[i] = z_code
-            z_planes[i] = z_plane
 
         def project(y):
-            b, half, t = y // 4, (y % 4) // 2, y % 2
-            outs = slice(t * P, (t + 1) * P)
+            b, half, part = y // 4, (y % 4) // 2, y % 2
+            cols = slice(part * Y_COLS, (part + 1) * Y_COLS)
             bank = wide_psum.tile([P, BANK], F32, tag="wide")
-            for g in range(PASSES):
-                i = 4 * b + 2 * half + g
-                nc.tensor.matmul_mx(
-                    out=bank[:],
-                    lhsT=w_words[:, g, outs].bitcast(FP8X4),
-                    lhsT_scale=w_plane[:, g, outs],
-                    rhs=z_codes[i][:].bitcast(FP8X4),
-                    rhs_scale=z_planes[i][:],
-                    start=(g == 0),
-                    stop=(g == PASSES - 1),
-                )
+            for t in range(OUT_CH // P):
+                outs = slice(t * P, (t + 1) * P)
+                for g in range(PASSES):
+                    i = 4 * b + 2 * half + g
+                    nc.tensor.matmul_mx(
+                        out=bank[:, t * Y_COLS : (t + 1) * Y_COLS],
+                        lhsT=w_words[:, g, outs].bitcast(FP8X4),
+                        lhsT_scale=w_plane[:, g, outs],
+                        rhs=z_codes[i][:, cols].bitcast(FP8X4),
+                        rhs_scale=z_planes[i][:, cols],
+                        start=(g == 0),
+                        stop=(g == PASSES - 1),
+                    )
             y_banks[y] = bank
 
         def finish(y):
-            b, half, t = y // 4, (y % 4) // 2, y % 2
-            cols = slice(half * BANK, (half + 1) * BANK)
-            result = result_pool.tile([P, BANK], F32)
-            nc.vector.scalar_tensor_tensor(
-                out=result[:],
-                in0=y_banks[y][:],
-                scalar=bias[:, t : t + 1],
-                in1=x_tiles[b][:, t, cols],
-                op0=ADD,
-                op1=ADD,
+            b = y // 4
+            cols = slice((y % 4) * Y_COLS, (y % 4 + 1) * Y_COLS)
+            result = result_pool.tile([P, OUT_CH // P, Y_COLS], F32)
+            for t in range(OUT_CH // P):
+                nc.vector.scalar_tensor_tensor(
+                    out=result[:, t, :],
+                    in0=y_banks[y][:, t * Y_COLS : (t + 1) * Y_COLS],
+                    scalar=bias[:, t : t + 1],
+                    in1=x_tiles[b][:, t, cols],
+                    op0=ADD,
+                    op1=ADD,
+                )
+            nc.sync.dma_start(
+                out=out_rows[b].rearrange("(t p) n -> p t n", p=P)[:, :, cols], in_=result[:]
             )
-            nc.sync.dma_start(out=out_rows[b, t * P : (t + 1) * P, cols], in_=result[:])
 
         ident_f32 = const.tile([P, P], F32)
         make_identity(nc, ident_f32[:])
@@ -211,17 +219,27 @@ def tile_soablock_pb_t_kernel(tc, attn, h_x, v_w_words, v_w_scales, v_b, x, out)
         bias = const.tile([P, OUT_CH // P], F32)
         nc.vector.tensor_copy(out=bias[:], in_=bias_bank[:, 0 : OUT_CH // P])
 
+        def quarters_to_transpose(i):
+            first = i + TRANSPOSE_AHEAD
+            if first >= QUARTERS:
+                return []
+            if first < 4:
+                return [first]
+            return [first, first + 1] if i % 2 == 0 else []
+
         for i in range(ROUNDS + PROJECT_BEHIND + 1):
             if i + LOAD_AHEAD < QUARTERS:
                 load_quarter(i + LOAD_AHEAD)
+            if 0 <= i - 1 < ROUNDS:
+                quantise_z(i - 1, 1)
+            for q in quarters_to_transpose(i):
+                transpose_quarter(q)
             if 0 <= i - PROJECT_BEHIND - 1 < Y_GROUPS:
                 finish(i - PROJECT_BEHIND - 1)
-            if 0 <= i - 1 < ROUNDS:
-                quantise_z(i - 1)
             if i + TRANSPOSE_AHEAD < QUARTERS:
-                transpose_quarter(i + TRANSPOSE_AHEAD)
                 quantise_quarter(i + TRANSPOSE_AHEAD)
             if i < ROUNDS:
                 mix_round(i)
+                quantise_z(i, 0)
             if 0 <= i - PROJECT_BEHIND < Y_GROUPS:
                 project(i - PROJECT_BEHIND)

@@ -219,21 +219,13 @@ def tile_soablock_pb_t_kernel(tc, attn, h_x, v_w_words, v_w_scales, v_b, x, out)
         bias = const.tile([P, OUT_CH // P], F32)
         nc.vector.tensor_copy(out=bias[:], in_=bias_bank[:, 0 : OUT_CH // P])
 
-        def quarters_to_transpose(i):
-            first = i + TRANSPOSE_AHEAD
-            if first >= QUARTERS:
-                return []
-            if first < 4:
-                return [first]
-            return [first, first + 1] if i % 2 == 0 else []
-
         for i in range(ROUNDS + PROJECT_BEHIND + 1):
             if i + LOAD_AHEAD < QUARTERS:
                 load_quarter(i + LOAD_AHEAD)
             if 0 <= i - 1 < ROUNDS:
                 quantise_z(i - 1, 1)
-            for q in quarters_to_transpose(i):
-                transpose_quarter(q)
+            if i + TRANSPOSE_AHEAD < QUARTERS:
+                transpose_quarter(i + TRANSPOSE_AHEAD)
             if 0 <= i - PROJECT_BEHIND - 1 < Y_GROUPS:
                 finish(i - PROJECT_BEHIND - 1)
             if i + TRANSPOSE_AHEAD < QUARTERS:

from contextlib import ExitStack

import concourse.mybir as mybir
from concourse.masks import make_identity

BF16 = mybir.dt.bfloat16
F32 = mybir.dt.float32
I32 = mybir.dt.int32
U32 = mybir.dt.uint32
U8 = mybir.dt.uint8
FP8X4 = mybir.dt.float8_e4m3fn_x4
ADD = mybir.AluOpType.add

BATCH = 4
OUT_CH = 256
MID_CH = 1024
POS = 1024

P = 128
PACK = 4
K_PASS = P * PACK
PASSES = POS // K_PASS
BANK = 512

QUARTER = 512
ROW_TILES = QUARTER // P
QUARTERS = 4 * BATCH
ROUNDS = 4 * BATCH
Y_GROUPS = 4 * BATCH
Y_COLS = POS // 4

TRANSPOSE_AHEAD = 2
LOAD_AHEAD = 6
PROJECT_BEHIND = 2

FLOPS = 2 * BATCH * (MID_CH * POS * POS + OUT_CH * MID_CH * POS)


def tile_soablock_pb_t_kernel(tc, attn, h_x, v_w_words, v_w_scales, v_b, x, out):
    nc = tc.nc
    x_rows = x.rearrange("b c h w -> b c (h w)")
    out_rows = out.rearrange("b c h w -> b c (h w)")

    with ExitStack() as stack:
        const = stack.enter_context(tc.tile_pool(name="const", bufs=1))
        raw_pool = stack.enter_context(tc.tile_pool(name="raw", bufs=LOAD_AHEAD + 2))
        grouped_pool = stack.enter_context(tc.tile_pool(name="grouped", bufs=2))
        codes_pool = stack.enter_context(tc.tile_pool(name="codes", bufs=6))
        z_grouped_pool = stack.enter_context(tc.tile_pool(name="z_grouped", bufs=2))
        z_codes_pool = stack.enter_context(tc.tile_pool(name="z_codes", bufs=4))
        x_pool = stack.enter_context(tc.tile_pool(name="x", bufs=3))
        result_pool = stack.enter_context(tc.tile_pool(name="result", bufs=3))
        z_psum = stack.enter_context(tc.psum_pool(name="z_psum", bufs=3))
        wide_psum = stack.enter_context(tc.psum_pool(name="wide_psum", bufs=5))
        stack.enter_context(tc.manual_schedule())

        raws, groupeds, codes, planes = {}, {}, {}, {}
        z_groupeds, z_codes, z_planes = {}, {}, {}
        x_tiles, y_banks = {}, {}

        def load_quarter(q):
            b, half = q // 4, (q % 4) // 2
            rows = slice(half * QUARTER, (half + 1) * QUARTER)
            if q % 2 == 0:
                source = h_x[b, rows, :].rearrange("(p j) m -> p j m", j=ROW_TILES)
            else:
                source = attn[b, rows, :].rearrange("(r p) m -> p r m", p=P)
            raw = raw_pool.tile([P, ROW_TILES, POS], BF16)
            for pair in range(ROW_TILES // 2):
                two = slice(2 * pair, 2 * pair + 2)
                nc.sync.dma_start(out=raw[:, two, :], in_=source[:, two, :])
            raws[q] = raw
            if q % 4 == 3:
                x_tile = x_pool.tile([P, OUT_CH // P, POS], BF16)
                nc.sync.dma_start(out=x_tile[:], in_=x_rows[b].rearrange("(t p) n -> p t n", p=P))
                x_tiles[b] = x_tile

        def transpose_quarter(q):
            raw = raws[q]
            grouped = grouped_pool.tile([P, PASSES, QUARTER, PACK], BF16, align_bytes=64)
            for pair in range(ROW_TILES // 2):
                for k in range(PASSES):
                    bank = wide_psum.tile([P, BANK], F32, tag="wide")
                    for u in range(2):
                        for r in range(2):
                            words = raw[:, 2 * pair + r, :].bitcast(F32)
                            first = (2 * k + u) * P
                            nc.tensor.transpose(
                                bank[:, (2 * u + r) * P : (2 * u + r + 1) * P],
                                words[:, first : first + P],
                                ident_f32[:],
                            )
                    rows = slice(2 * pair * P, (2 * pair + 2) * P)
                    dest = grouped[:, k, rows, :].bitcast(F32)
                    source = bank[:].rearrange("p (u r) -> p r u", u=2)
                    if k == 0:
                        nc.scalar.copy(out=dest, in_=source)
                    else:
                        nc.vector.tensor_copy(out=dest, in_=source)
            groupeds[q] = grouped

        def quantise_quarter(q):
            grouped = groupeds[q]
            code = codes_pool.tile([P, PASSES, QUARTER], U32, align_bytes=64)
            plane = codes_pool.tile([P, PASSES, QUARTER], U8, align_bytes=64)
            for k in range(PASSES):
                nc.vector.quantize_mx(
                    out=code[:, k, :].bitcast(FP8X4),
                    scales=plane[:, k, :],
                    in_=grouped[:, k, :, :].rearrange("p r t -> p (r t)"),
                )
            codes[q] = code
            planes[q] = plane

        def mix_round(i):
            b, half, g = i // 4, (i % 4) // 2, i % 2
            h_q, a_q = 4 * b + 2 * g, 4 * b + 2 * half + 1
            z_grouped = z_grouped_pool.tile([P, QUARTER, PACK], BF16, align_bytes=64)
            for chunk in range(QUARTER // P):
                cols = slice(chunk * P, (chunk + 1) * P)
                bank = z_psum.tile([P, PACK, P], F32)
                for j in range(PACK):
                    chans = slice(j * P, (j + 1) * P)
                    for k in range(PASSES):
                        nc.tensor.matmul_mx(
                            out=bank[:, j, :],
                            lhsT=codes[h_q][:, k, chans].bitcast(FP8X4),
                            lhsT_scale=planes[h_q][:, k, chans],
                            rhs=codes[a_q][:, k, cols].bitcast(FP8X4),
                            rhs_scale=planes[a_q][:, k, cols],
                            start=(k == 0),
                            stop=(k == PASSES - 1),
                        )
                nc.scalar.copy(out=z_grouped[:, cols, :], in_=bank[:].rearrange("p j n -> p n j"))
            z_groupeds[i] = z_grouped

        def quantise_z(i, part):
            if part == 0:
                z_code = z_codes_pool.tile([P, QUARTER], U32, align_bytes=64)
                z_plane = z_codes_pool.tile([P, QUARTER], U8, align_bytes=64)
                z_codes[i] = z_code
                z_planes[i] = z_plane
            cols = slice(part * Y_COLS, (part + 1) * Y_COLS)
            nc.vector.quantize_mx(
                out=z_codes[i][:, cols].bitcast(FP8X4),
                scales=z_planes[i][:, cols],
                in_=z_groupeds[i][:, cols, :].rearrange("p n j -> p (n j)"),
            )

        def project(y):
            b, half, part = y // 4, (y % 4) // 2, y % 2
            cols = slice(part * Y_COLS, (part + 1) * Y_COLS)
            bank = wide_psum.tile([P, BANK], F32, tag="wide")
            for t in range(OUT_CH // P):
                outs = slice(t * P, (t + 1) * P)
                for g in range(PASSES):
                    i = 4 * b + 2 * half + g
                    nc.tensor.matmul_mx(
                        out=bank[:, t * Y_COLS : (t + 1) * Y_COLS],
                        lhsT=w_words[:, g, outs].bitcast(FP8X4),
                        lhsT_scale=w_plane[:, g, outs],
                        rhs=z_codes[i][:, cols].bitcast(FP8X4),
                        rhs_scale=z_planes[i][:, cols],
                        start=(g == 0),
                        stop=(g == PASSES - 1),
                    )
            y_banks[y] = bank

        def finish(y):
            b = y // 4
            cols = slice((y % 4) * Y_COLS, (y % 4 + 1) * Y_COLS)
            result = result_pool.tile([P, OUT_CH // P, Y_COLS], F32)
            for t in range(OUT_CH // P):
                nc.vector.scalar_tensor_tensor(
                    out=result[:, t, :],
                    in0=y_banks[y][:, t * Y_COLS : (t + 1) * Y_COLS],
                    scalar=bias[:, t : t + 1],
                    in1=x_tiles[b][:, t, cols],
                    op0=ADD,
                    op1=ADD,
                )
            nc.sync.dma_start(
                out=out_rows[b].rearrange("(t p) n -> p t n", p=P)[:, :, cols], in_=result[:]
            )

        ident_f32 = const.tile([P, P], F32)
        make_identity(nc, ident_f32[:])
        ident_bf16 = const.tile([P, P], BF16)
        make_identity(nc, ident_bf16[:])

        w_words = const.tile([P, PASSES, OUT_CH], U32, align_bytes=64)
        w_plane = const.tile([P, PASSES, OUT_CH], U8, align_bytes=64)
        nc.vector.memset(w_plane[:].bitcast(I32), 0)
        bias_rows = const.tile([P, P], BF16)
        nc.vector.memset(bias_rows[:], 0.0)

        load_quarter(0)
        load_quarter(1)
        nc.sync.dma_start(out=bias_rows[0 : OUT_CH // P, :], in_=v_b.rearrange("(t p) -> t p", p=P))
        load_quarter(2)
        nc.sync.dma_start(
            out=w_words[:].bitcast(I32),
            in_=v_w_words.rearrange("g p o t -> p g (o t)").bitcast(I32),
        )
        for quad in range(4):
            nc.sync.dma_start(
                out=w_plane[32 * quad : 32 * quad + 4, :, :].bitcast(I32),
                in_=v_w_scales[:, 4 * quad : 4 * quad + 4, :].rearrange("g r o -> r g o").bitcast(I32),
            )
        for q in range(3, LOAD_AHEAD):
            load_quarter(q)

        for q in range(TRANSPOSE_AHEAD):
            transpose_quarter(q)
            quantise_quarter(q)

        bias_bank = wide_psum.tile([P, P], BF16, tag="wide")
        nc.tensor.transpose(bias_bank[:], bias_rows[:], ident_bf16[:])
        bias = const.tile([P, OUT_CH // P], F32)
        nc.vector.tensor_copy(out=bias[:], in_=bias_bank[:, 0 : OUT_CH // P])

        for i in range(ROUNDS + PROJECT_BEHIND + 1):
            if i + LOAD_AHEAD < QUARTERS:
                load_quarter(i + LOAD_AHEAD)
            if 0 <= i - 1 < ROUNDS:
                quantise_z(i - 1, 1)
            if i + TRANSPOSE_AHEAD < QUARTERS:
                transpose_quarter(i + TRANSPOSE_AHEAD)
            if 0 <= i - PROJECT_BEHIND - 1 < Y_GROUPS:
                finish(i - PROJECT_BEHIND - 1)
            if i + TRANSPOSE_AHEAD < QUARTERS:
                quantise_quarter(i + TRANSPOSE_AHEAD)
            if i < ROUNDS:
                mix_round(i)
                quantise_z(i, 0)
            if 0 <= i - PROJECT_BEHIND < Y_GROUPS:
                project(i - PROJECT_BEHIND)
